import numpy as np
import ml_dtypes


def mxq(x, axis, fmt="e4m3"):
    dtype, down = {"e4m3": (ml_dtypes.float8_e4m3fn, 7), "e5m2": (ml_dtypes.float8_e5m2, 14)}[fmt]
    v = np.moveaxis(np.asarray(x, np.float32).astype(ml_dtypes.bfloat16).astype(np.float64), axis, -1)
    blocks = v.reshape(v.shape[:-1] + (-1, 32))
    amax = np.abs(blocks).max(-1, keepdims=True)
    byte = np.maximum(np.where(amax > 0, np.frexp(amax)[1] - 1 + 127, 0) - down, 1)
    scale = np.exp2(byte - 127.0)
    codes = (blocks / scale).astype(np.float32).astype(dtype).astype(np.float64)
    return np.moveaxis((codes * scale).reshape(v.shape), -1, axis)


WIDE = False


def mx_kscale(k):
    if not WIDE:
        return np.ones(k)
    levels = np.array([10, -10, 5, -5, 0])
    if k % 512:
        return np.exp2(np.random.permutation(np.resize(levels, k // 32))).repeat(32)
    a = np.empty((k // 512, 16))
    for p in range(k // 512):
        a[p, :8] = np.random.permutation(np.resize(levels, 8))
        for g in range(8):
            far = levels[np.abs(levels - a[p, g]) >= 10]
            a[p, g + 8] = far[np.random.randint(len(far))]
    return np.exp2(a.ravel()).repeat(32)


BF16 = ml_dtypes.bfloat16


def bf(x):
    return np.asarray(x, np.float32).astype(BF16)


def f64(x):
    return np.asarray(x).astype(np.float64)


BATCH, IN_F, OUT_F, RANK, N_ADAPTERS = 1024, 2048, 2048, 128, 8
SEG = BATCH // N_ADAPTERS
LORA_GAIN = 2.0


def draw0():
    s = mx_kscale(IN_F)
    return {"x": bf(np.random.standard_normal((BATCH, IN_F)) * s),
            "h_lora": bf(np.random.standard_normal((N_ADAPTERS, SEG, RANK))),
            "lora_B": bf(np.random.standard_normal((N_ADAPTERS, RANK, OUT_F)) * 0.5 / np.sqrt(RANK)),
            "M": bf(np.random.standard_normal((IN_F, OUT_F)) / np.sqrt(IN_F) / s[:, None])}


def core(x, h_lora, lora_B, M):
    y = (f64(h_lora) @ f64(lora_B)) * LORA_GAIN
    y = y.reshape(BATCH, OUT_F)
    return y + (mxq(f64(x), 1, "e4m3") @ mxq(f64(M), 0, "e4m3"))


def e4m3fn_bytes(y):
    return np.clip(np.asarray(y, np.float64), -448.0, 448.0).astype(np.float32).astype(ml_dtypes.float8_e4m3fn).view(np.uint8)


def e4m3fn_values(b):
    return np.asarray(b, np.uint8).view(ml_dtypes.float8_e4m3fn).astype(np.float64)


def setup_inputs():
    d = draw0()
    x0 = np.asarray(d['M']).astype(np.float64)
    s = (np.max(np.abs(x0), axis=(1,), keepdims=True) / 448.0).astype(np.float32)
    out = {}
    for k, v in d.items():
        if k == 'M':
            out['M_bytes'] = e4m3fn_bytes(x0 / s.astype(np.float64))
            out['M_scale'] = s
        else:
            out[k] = v
    return out


def reference(x, h_lora, lora_B, M_bytes, M_scale):
    return core(x, h_lora, lora_B, e4m3fn_values(M_bytes) * M_scale.astype(np.float64))

@@ -1,0 +1,278 @@
+from contextlib import ExitStack
+
+import concourse.mybir as mybir
+from concourse.masks import make_identity
+
+BATCH, IN_F, OUT_F, RANK, N_AD = 1024, 2048, 2048, 128, 8
+FLOPS = 2 * BATCH * IN_F * OUT_F + 2 * BATCH * RANK * OUT_F
+
+F32 = mybir.dt.float32
+BF16 = mybir.dt.bfloat16
+U32 = mybir.dt.uint32
+U8 = mybir.dt.uint8
+FP8 = mybir.dt.float8_e4m3fn
+FP8X4 = mybir.dt.float8_e4m3fn_x4
+COPY = mybir.ActivationFunctionType.Copy
+MULT = mybir.AluOpType.mult
+ADD = mybir.AluOpType.add
+
+P = 128
+PACK = 4
+K_PASS = P * PACK
+N_PASS = IN_F // K_PASS
+LW = 512
+N_M = BATCH // P
+
+WIDTHS = (512, 512, 512, 256, 256)
+V_PLANES = (4, 2, 0, 2, 4)
+S_INTER = (0, 0, 0, 0, 0)
+X_EVAC_V = 4
+L_EVAC_V = (0, 0, 0, 0, 0)
+SH_S = 3
+SH_V = 1
+X_LEAD = 5
+L_LEAD = 0
+LAG_LE = 1
+LAG_F = 2
+D_LEAD = {"m": 6, "x": 6, "b": 6, "h": 6}
+B_SPLIT = 2
+FAST_INTER = True
+MANUAL = True
+
+
+def spread(total, n):
+    return [(total * (i + 1)) // n - (total * i) // n for i in range(n)]
+
+
+def tile_lorasequential_pa_kernel(tc, x, h_lora, lora_B, M_bytes, M_scale, out):
+    nc = tc.nc
+    n_ch = len(WIDTHS)
+    n_u = N_M * n_ch
+    offs = [sum(WIDTHS[:i]) for i in range(n_ch)]
+    v_plane = []
+    s_int = []
+    l_vec = []
+    for j in range(n_ch):
+        v_plane.extend(spread(V_PLANES[j], N_PASS * PACK))
+        s_int.extend(spread(S_INTER[j], N_PASS))
+        l_vec.extend(spread(L_EVAC_V[j], N_M))
+    x_vec = spread(X_EVAC_V, 2 * N_M)
+    with ExitStack() as ctx:
+        const = ctx.enter_context(tc.tile_pool(name="const", bufs=1))
+        loads = ctx.enter_context(tc.tile_pool(name="loads", bufs=1))
+        codes = ctx.enter_context(tc.tile_pool(name="codes", bufs=1))
+        work = ctx.enter_context(tc.tile_pool(name="work", bufs=3))
+        psum = ctx.enter_context(tc.psum_pool(name="psum", bufs=4))
+        if MANUAL:
+            ctx.enter_context(tc.manual_schedule())
+
+        ident_f = const.tile([P, P], F32, name="ident_f")
+        make_identity(nc, ident_f[:])
+        ident_b = const.tile([P, P], BF16, name="ident_b")
+        make_identity(nc, ident_b[:])
+        warm = const.tile([P, 2], F32, name="warm")
+        nc.vector.memset(warm[:, 0:1], 0.0)
+        nc.scalar.activation(out=warm[:, 1:2], in_=warm[:, 0:1], func=COPY)
+
+        msc = const.tile([P, N_PASS, PACK], F32, name="msc")
+        nc.sync.dma_start(out=msc[:], in_=M_scale.rearrange("(g p t) o -> p g (t o)", p=P, t=PACK))
+        m_view = M_bytes.rearrange("(g p t) n -> g p t n", p=P, t=PACK)
+        b_view = lora_B.rearrange("a r n -> r a n")
+        mb = {}
+        xin = {}
+        lb = {}
+        hin = loads.tile([P, N_AD, RANK], BF16, name="hin")
+        hT = codes.tile([P, N_AD, P], BF16, name="hT")
+
+        def load(item):
+            kind = item[0]
+            if kind == "m":
+                jl, g = item[1], item[2]
+                t = loads.tile([P, PACK, LW], U8, name="mb%d_%d" % (jl, g))
+                nc.sync.dma_start(out=t[:], in_=m_view[g][:, :, jl * LW:(jl + 1) * LW])
+                mb[(jl, g)] = t
+            elif kind == "x":
+                m = item[1]
+                t = loads.tile([P, IN_F], BF16, name="xin%d" % m)
+                nc.sync.dma_start(out=t[:], in_=x[m * P:(m + 1) * P, :])
+                xin[m] = t
+            elif kind == "b":
+                jl, a0 = item[1], item[2]
+                t = loads.tile([P, B_SPLIT, LW], BF16, name="lb%d_%d" % (jl, a0))
+                nc.sync.dma_start(out=t[:], in_=b_view[:, a0:a0 + B_SPLIT, jl * LW:(jl + 1) * LW])
+                lb[(jl, a0)] = t
+            else:
+                nc.sync.dma_start(out=hin[:], in_=h_lora.rearrange("a b r -> b a r"))
+
+        wide = {}
+        grp = {}
+        mc = {}
+        ms = {}
+        xc = {}
+        xs = {}
+        xg = {}
+        tps = {}
+        lps = {}
+        lo = {}
+        acc = {}
+
+        def wid(s, t):
+            j, g = divmod(s, N_PASS)
+            w = WIDTHS[j]
+            jl, c0 = divmod(offs[j], LW)
+            if s not in wide:
+                wt = work.tile([P, PACK, w], BF16, name="wide", tag="wide", bufs=3)
+                wide[s] = wt
+            dst = wide[s][:, t, :]
+            src = mb[(jl, g)][:, t, c0:c0 + w].bitcast(FP8)
+            if v_plane[j * N_PASS * PACK + g * PACK + t]:
+                nc.vector.tensor_scalar(out=dst, in0=src, scalar1=msc[:, g, t:t + 1], scalar2=None, op0=MULT)
+            else:
+                nc.scalar.activation(out=dst, in_=src, func=COPY, scale=msc[:, g, t:t + 1])
+
+        def itl(s):
+            w = WIDTHS[s // N_PASS]
+            gt = work.tile([P, w, PACK], BF16, name="grp", tag="grp", bufs=3, align_bytes=64)
+            if FAST_INTER:
+                dst = gt[:].rearrange("p (c i) t -> p c t i", i=4)
+                src = wide[s][:].rearrange("p t (c i) -> p c t i", i=4)
+            else:
+                dst = gt[:]
+                src = wide[s][:].rearrange("p t n -> p n t")
+            if s_int[s]:
+                nc.scalar.copy(out=dst, in_=src)
+            else:
+                nc.vector.tensor_copy(out=dst, in_=src)
+            grp[s] = gt
+
+        def qnt(s):
+            w = WIDTHS[s // N_PASS]
+            c = codes.tile([P, w], U32, name="mc%d" % s, align_bytes=64)
+            sc = codes.tile([P, w], U8, name="ms%d" % s, align_bytes=64)
+            nc.vector.quantize_mx(out=c[:].bitcast(FP8X4), scales=sc[:],
+                                  in_=grp[s][:].rearrange("p n t -> p (n t)"))
+            mc[s] = c
+            ms[s] = sc
+
+        def x_tr(m, hh):
+            words = xin[m][:].bitcast(F32)
+            tp = psum.tile([P, 2, 2, P], F32, name="tp", tag="aux", bufs=4)
+            for gi in range(2):
+                g = 2 * hh + gi
+                for u in range(2):
+                    nc.tensor.transpose(tp[:, gi, u, :], words[:, 256 * g + u:256 * (g + 1):2], ident_f[:])
+            tps[(m, hh)] = tp
+
+        def x_ev(m, hh):
+            if m not in xg:
+                gw = work.tile([P, N_PASS, P, 2], F32, name="xg", tag="xg", bufs=3, align_bytes=64)
+                xg[m] = gw
+            dst = xg[m][:, 2 * hh:2 * hh + 2, :, :]
+            src = tps[(m, hh)][:].rearrange("p g u r -> p g r u")
+            if x_vec[2 * m + hh]:
+                nc.vector.tensor_copy(out=dst, in_=src)
+            else:
+                nc.scalar.copy(out=dst, in_=src)
+
+        def x_q(m):
+            c = codes.tile([P, N_PASS * P], U32, name="xc%d" % m, align_bytes=64)
+            sc = codes.tile([P, N_PASS * P], U8, name="xs%d" % m, align_bytes=64)
+            nc.vector.quantize_mx(out=c[:].bitcast(FP8X4), scales=sc[:],
+                                  in_=xg[m][:].rearrange("p g r u -> p (g r u)").bitcast(BF16))
+            xc[m] = c
+            xs[m] = sc
+
+        def h_tr():
+            tp = psum.tile([P, N_AD, P], BF16, name="tph", tag="aux", bufs=4)
+            for a in range(N_AD):
+                nc.tensor.transpose(tp[:, a, :], hin[:, a, :], ident_b[:])
+            nc.vector.tensor_copy(out=hT[:], in_=tp[:])
+
+        def l_mm(u):
+            j, m = divmod(u, N_M)
+            w = WIDTHS[j]
+            jl, c0 = divmod(offs[j], LW)
+            lp = psum.tile([P, w], F32, name="lp", tag="aux", bufs=4)
+            nc.tensor.matmul(lp[:], lhsT=hT[:, m, :], rhs=lb[(jl, m - m % B_SPLIT)][:, m % B_SPLIT, c0:c0 + w], start=True, stop=True)
+            lps[u] = lp
+
+        def l_ev(u):
+            w = WIDTHS[u // N_M]
+            l = work.tile([P, w], F32, name="lo", tag="lo", bufs=10)
+            if l_vec[u]:
+                nc.vector.tensor_scalar(out=l[:], in0=lps[u][:], scalar1=2.0, scalar2=None, op0=MULT)
+            else:
+                nc.scalar.activation(out=l[:], in_=lps[u][:], func=COPY, scale=2.0)
+            lo[u] = l
+
+        def mx(u):
+            j, m = divmod(u, N_M)
+            a = psum.tile([P, WIDTHS[j]], F32, name="acc", tag="acc", bufs=4)
+            for g in range(N_PASS):
+                s = j * N_PASS + g
+                cols = slice(g * P, (g + 1) * P)
+                nc.tensor.matmul_mx(out=a[:],
+                                    lhsT=xc[m][:, cols].bitcast(FP8X4), lhsT_scale=xs[m][:, cols],
+                                    rhs=mc[s][:].bitcast(FP8X4), rhs_scale=ms[s][:],
+                                    start=(g == 0), stop=(g == N_PASS - 1))
+            acc[u] = a
+
+        def fin(u):
+            j, m = divmod(u, N_M)
+            l = lo[u]
+            nc.vector.tensor_tensor(out=l[:], in0=acc[u][:], in1=l[:], op=ADD)
+            nc.sync.dma_start(out=out[m * P:(m + 1) * P, offs[j]:offs[j] + WIDTHS[j]], in_=l[:])
+
+        need = []
+        for j in range(n_ch):
+            for g in range(N_PASS):
+                need.append((N_M * j + 2 * g - N_M - SH_S - D_LEAD["m"], 0, ("m", offs[j] // LW, g)))
+            for a0 in range(0, N_AD, B_SPLIT):
+                need.append((N_M * j + a0 - L_LEAD - D_LEAD["b"], 2, ("b", offs[j] // LW, a0)))
+        for m in range(N_M):
+            need.append((m - X_LEAD - D_LEAD["x"], 1, ("x", m)))
+        need.append((min(-L_LEAD, 0) - 2 - D_LEAD["h"], 1, ("h",)))
+        sched = []
+        seen = set()
+        for slot, rank, item in sorted(need, key=lambda z: (z[0], z[1])):
+            if item not in seen:
+                seen.add(item)
+                sched.append((slot, item))
+
+        first = min(-N_M - SH_S, -X_LEAD, -L_LEAD - 3, -3)
+        n_loaded = 0
+        for sl in range(first, n_u + LAG_F + LAG_LE + max(0, -L_LEAD) + 2):
+            while n_loaded < len(sched) and sched[n_loaded][0] <= sl:
+                load(sched[n_loaded][1])
+                n_loaded += 1
+            m = sl + X_LEAD
+            if 0 <= m < N_M:
+                x_tr(m, 0)
+                x_tr(m, 1)
+            if sl == min(-L_LEAD, 0) - 2:
+                h_tr()
+            if 0 <= sl + L_LEAD < n_u:
+                l_mm(sl + L_LEAD)
+            if 0 <= sl < n_u:
+                mx(sl)
+            if 0 <= m < N_M:
+                x_ev(m, 0)
+                x_ev(m, 1)
+            if 0 <= sl + L_LEAD - LAG_LE < n_u:
+                l_ev(sl + L_LEAD - LAG_LE)
+            if 0 <= sl - LAG_F < n_u:
+                fin(sl - LAG_F)
+            q = sl + N_M + SH_S
+            if 0 <= q < n_u:
+                j, i = divmod(q, N_M)
+                wid(N_PASS * j + i // 2, 2 * (i % 2))
+                wid(N_PASS * j + i // 2, 2 * (i % 2) + 1)
+            q = sl + N_M + SH_V
+            if 0 <= q < n_u:
+                j, i = divmod(q, N_M)
+                if i % 2 == 0:
+                    itl(N_PASS * j + i // 2)
+                else:
+                    qnt(N_PASS * j + i // 2)
+            if 0 <= m - 1 < N_M:
+                x_q(m - 1)

@@ -30,11 +30,11 @@ X_EVAC_V = 4
 L_EVAC_V = (0, 0, 0, 0, 0)
 SH_S = 3
 SH_V = 1
-X_LEAD = 5
+X_LEAD = 7
 L_LEAD = 0
 LAG_LE = 1
 LAG_F = 2
-D_LEAD = {"m": 6, "x": 6, "b": 6, "h": 6}
+D_LEAD = {"m": 4, "x": 6, "b": 6, "h": 6}
 B_SPLIT = 2
 FAST_INTER = True
 MANUAL = True

@@ -74,8 +74,10 @@ def tile_lorasequential_pa_kernel(tc, x, h_lora, lora_B, M_bytes, M_scale, out):
         nc.vector.memset(warm[:, 0:1], 0.0)
         nc.scalar.activation(out=warm[:, 1:2], in_=warm[:, 0:1], func=COPY)
 
-        msc = const.tile([P, N_PASS, PACK], F32, name="msc")
-        nc.sync.dma_start(out=msc[:], in_=M_scale.rearrange("(g p t) o -> p g (t o)", p=P, t=PACK))
+        msc_first = const.tile([P, PACK], F32, name="msc_first")
+        msc_rest = const.tile([P, N_PASS - 1, PACK], F32, name="msc_rest")
+        sc_view = M_scale.rearrange("(g p t) o -> p g (t o)", p=P, t=PACK)
+        nc.sync.dma_start(out=msc_first[:], in_=sc_view[:, 0, :])
         m_view = M_bytes.rearrange("(g p t) n -> g p t n", p=P, t=PACK)
         b_view = lora_B.rearrange("a r n -> r a n")
         mb = {}
@@ -88,9 +90,14 @@ def tile_lorasequential_pa_kernel(tc, x, h_lora, lora_B, M_bytes, M_scale, out):
             kind = item[0]
             if kind == "m":
                 jl, g = item[1], item[2]
-                t = loads.tile([P, PACK, LW], U8, name="mb%d_%d" % (jl, g))
-                nc.sync.dma_start(out=t[:], in_=m_view[g][:, :, jl * LW:(jl + 1) * LW])
-                mb[(jl, g)] = t
+                n = 1 if (jl, g) == (0, 0) else PACK
+                for t0 in range(0, PACK, n):
+                    t = loads.tile([P, n, LW], U8, name="mb%d_%d_%d" % (jl, g, t0))
+                    nc.sync.dma_start(out=t[:], in_=m_view[g][:, t0:t0 + n, jl * LW:(jl + 1) * LW])
+                    for i in range(n):
+                        mb[(jl, g, t0 + i)] = t[:, i, :]
+                if (jl, g) == (0, 0):
+                    nc.sync.dma_start(out=msc_rest[:], in_=sc_view[:, 1:, :])
             elif kind == "x":
                 m = item[1]
                 t = loads.tile([P, IN_F], BF16, name="xin%d" % m)
@@ -124,11 +131,12 @@ def tile_lorasequential_pa_kernel(tc, x, h_lora, lora_B, M_bytes, M_scale, out):
                 wt = work.tile([P, PACK, w], BF16, name="wide", tag="wide", bufs=3)
                 wide[s] = wt
             dst = wide[s][:, t, :]
-            src = mb[(jl, g)][:, t, c0:c0 + w].bitcast(FP8)
+            src = mb[(jl, g, t)][:, c0:c0 + w].bitcast(FP8)
+            scale = msc_first[:, t:t + 1] if g == 0 else msc_rest[:, g - 1, t:t + 1]
             if v_plane[j * N_PASS * PACK + g * PACK + t]:
-                nc.vector.tensor_scalar(out=dst, in0=src, scalar1=msc[:, g, t:t + 1], scalar2=None, op0=MULT)
+                nc.vector.tensor_scalar(out=dst, in0=src, scalar1=scale, scalar2=None, op0=MULT)
             else:
-                nc.scalar.activation(out=dst, in_=src, func=COPY, scale=msc[:, g, t:t + 1])
+                nc.scalar.activation(out=dst, in_=src, func=COPY, scale=scale)
 
         def itl(s):
             w = WIDTHS[s // N_PASS]

@@ -24,17 +24,18 @@ LW = 512
 N_M = BATCH // P
 
 WIDTHS = (512, 512, 512, 256, 256)
-V_PLANES = (4, 2, 0, 2, 4)
+V_PLANES = (8, 4, 0, 0, 2)
 S_INTER = (0, 0, 0, 0, 0)
-X_EVAC_V = 4
+X_EVAC_V = 0
 L_EVAC_V = (0, 0, 0, 0, 0)
 SH_S = 3
 SH_V = 1
-X_LEAD = 7
-L_LEAD = 0
+X_LEAD = 4
 LAG_LE = 1
 LAG_F = 2
-D_LEAD = {"m": 4, "x": 6, "b": 6, "h": 6}
+D_LEAD = {"m": 6, "x": 6, "b": 5, "h": 6}
+M_LATE = (0, 2, 0, 0, 0)
+L_LATE = 4
 B_SPLIT = 2
 FAST_INTER = True
 MANUAL = True
@@ -173,7 +174,7 @@ def tile_lorasequential_pa_kernel(tc, x, h_lora, lora_B, M_bytes, M_scale, out):
 
         def x_ev(m, hh):
             if m not in xg:
-                gw = work.tile([P, N_PASS, P, 2], F32, name="xg", tag="xg", bufs=3, align_bytes=64)
+                gw = work.tile([P, N_PASS, P, 2], F32, name="xg", tag="xg", bufs=4, align_bytes=64)
                 xg[m] = gw
             dst = xg[m][:, 2 * hh:2 * hh + 2, :, :]
             src = tps[(m, hh)][:].rearrange("p g u r -> p g r u")
@@ -234,12 +235,12 @@ def tile_lorasequential_pa_kernel(tc, x, h_lora, lora_B, M_bytes, M_scale, out):
         need = []
         for j in range(n_ch):
             for g in range(N_PASS):
-                need.append((N_M * j + 2 * g - N_M - SH_S - D_LEAD["m"], 0, ("m", offs[j] // LW, g)))
+                need.append((N_M * j + 2 * g - N_M - SH_S - D_LEAD["m"] + M_LATE[j], 0, ("m", offs[j] // LW, g)))
             for a0 in range(0, N_AD, B_SPLIT):
-                need.append((N_M * j + a0 - L_LEAD - D_LEAD["b"], 2, ("b", offs[j] // LW, a0)))
+                need.append((N_M * j + a0 - D_LEAD["b"], 2, ("b", offs[j] // LW, a0)))
         for m in range(N_M):
             need.append((m - X_LEAD - D_LEAD["x"], 1, ("x", m)))
-        need.append((min(-L_LEAD, 0) - 2 - D_LEAD["h"], 1, ("h",)))
+        need.append((-D_LEAD["h"], 1, ("h",)))
         sched = []
         seen = set()
         for slot, rank, item in sorted(need, key=lambda z: (z[0], z[1])):
@@ -247,9 +248,9 @@ def tile_lorasequential_pa_kernel(tc, x, h_lora, lora_B, M_bytes, M_scale, out):
                 seen.add(item)
                 sched.append((slot, item))
 
-        first = min(-N_M - SH_S, -X_LEAD, -L_LEAD - 3, -3)
+        first = min(-N_M - SH_S, -X_LEAD)
         n_loaded = 0
-        for sl in range(first, n_u + LAG_F + LAG_LE + max(0, -L_LEAD) + 2):
+        for sl in range(first, n_u + LAG_F + LAG_LE):
             while n_loaded < len(sched) and sched[n_loaded][0] <= sl:
                 load(sched[n_loaded][1])
                 n_loaded += 1
@@ -257,17 +258,19 @@ def tile_lorasequential_pa_kernel(tc, x, h_lora, lora_B, M_bytes, M_scale, out):
             if 0 <= m < N_M:
                 x_tr(m, 0)
                 x_tr(m, 1)
-            if sl == min(-L_LEAD, 0) - 2:
-                h_tr()
-            if 0 <= sl + L_LEAD < n_u:
-                l_mm(sl + L_LEAD)
+            if 0 <= sl - 1 < L_LATE:
+                l_mm(sl - 1)
+            if L_LATE <= sl < n_u:
+                l_mm(sl)
             if 0 <= sl < n_u:
                 mx(sl)
+            if sl == 0:
+                h_tr()
             if 0 <= m < N_M:
                 x_ev(m, 0)
                 x_ev(m, 1)
-            if 0 <= sl + L_LEAD - LAG_LE < n_u:
-                l_ev(sl + L_LEAD - LAG_LE)
+            if 0 <= sl - LAG_LE < n_u:
+                l_ev(sl - LAG_LE)
             if 0 <= sl - LAG_F < n_u:
                 fin(sl - LAG_F)
             q = sl + N_M + SH_S

@@ -91,7 +91,7 @@ def tile_lorasequential_pa_kernel(tc, x, h_lora, lora_B, M_bytes, M_scale, out):
             kind = item[0]
             if kind == "m":
                 jl, g = item[1], item[2]
-                n = 1 if (jl, g) == (0, 0) else PACK
+                n = PACK // 2 if jl == 0 else PACK
                 for t0 in range(0, PACK, n):
                     t = loads.tile([P, n, LW], U8, name="mb%d_%d_%d" % (jl, g, t0))
                     nc.sync.dma_start(out=t[:], in_=m_view[g][:, t0:t0 + n, jl * LW:(jl + 1) * LW])
@@ -214,23 +214,30 @@ def tile_lorasequential_pa_kernel(tc, x, h_lora, lora_B, M_bytes, M_scale, out):
                 nc.scalar.activation(out=l[:], in_=lps[u][:], func=COPY, scale=2.0)
             lo[u] = l
 
+        def parts(u):
+            w = WIDTHS[u // N_M]
+            n = w // 2 if u == n_u - 1 else w
+            return [slice(c, c + n) for c in range(0, w, n)]
+
         def mx(u):
             j, m = divmod(u, N_M)
             a = psum.tile([P, WIDTHS[j]], F32, name="acc", tag="acc", bufs=4)
-            for g in range(N_PASS):
-                s = j * N_PASS + g
-                cols = slice(g * P, (g + 1) * P)
-                nc.tensor.matmul_mx(out=a[:],
-                                    lhsT=xc[m][:, cols].bitcast(FP8X4), lhsT_scale=xs[m][:, cols],
-                                    rhs=mc[s][:].bitcast(FP8X4), rhs_scale=ms[s][:],
-                                    start=(g == 0), stop=(g == N_PASS - 1))
+            for c in parts(u):
+                for g in range(N_PASS):
+                    s = j * N_PASS + g
+                    cols = slice(g * P, (g + 1) * P)
+                    nc.tensor.matmul_mx(out=a[:, c],
+                                        lhsT=xc[m][:, cols].bitcast(FP8X4), lhsT_scale=xs[m][:, cols],
+                                        rhs=mc[s][:, c].bitcast(FP8X4), rhs_scale=ms[s][:, c],
+                                        start=(g == 0), stop=(g == N_PASS - 1))
             acc[u] = a
 
         def fin(u):
             j, m = divmod(u, N_M)
             l = lo[u]
-            nc.vector.tensor_tensor(out=l[:], in0=acc[u][:], in1=l[:], op=ADD)
-            nc.sync.dma_start(out=out[m * P:(m + 1) * P, offs[j]:offs[j] + WIDTHS[j]], in_=l[:])
+            for c in parts(u):
+                nc.vector.tensor_tensor(out=l[:, c], in0=acc[u][:, c], in1=l[:, c], op=ADD)
+                nc.sync.dma_start(out=out[m * P:(m + 1) * P, offs[j] + c.start:offs[j] + c.stop], in_=l[:, c])
 
         need = []
         for j in range(n_ch):

@@ -39,6 +39,7 @@ L_LATE = 4
 B_SPLIT = 2
 FAST_INTER = True
 MANUAL = True
+WARM_X = (2, 3, 4,)
 
 
 def spread(total, n):
@@ -163,6 +164,11 @@ def tile_lorasequential_pa_kernel(tc, x, h_lora, lora_B, M_bytes, M_scale, out):
             mc[s] = c
             ms[s] = sc
 
+        def warm_pe(m):
+            for i in range(2):
+                d = psum.tile([P, LW], F32, name="wp", tag="acc", bufs=4)
+                nc.tensor.matmul(d[:], lhsT=ident_b[:], rhs=xin[m - 1][:, i * LW:(i + 1) * LW], start=True, stop=True)
+
         def x_tr(m, hh):
             words = xin[m][:].bitcast(F32)
             tp = psum.tile([P, 2, 2, P], F32, name="tp", tag="aux", bufs=4)
@@ -263,6 +269,8 @@ def tile_lorasequential_pa_kernel(tc, x, h_lora, lora_B, M_bytes, M_scale, out):
                 n_loaded += 1
             m = sl + X_LEAD
             if 0 <= m < N_M:
+                if m in WARM_X:
+                    warm_pe(m)
                 x_tr(m, 0)
                 x_tr(m, 1)
             if 0 <= sl - 1 < L_LATE:

@@ -144,8 +144,8 @@ def tile_lorasequential_pa_kernel(tc, x, h_lora, lora_B, M_bytes, M_scale, out):
             w = WIDTHS[s // N_PASS]
             gt = work.tile([P, w, PACK], BF16, name="grp", tag="grp", bufs=3, align_bytes=64)
             if FAST_INTER:
-                dst = gt[:].rearrange("p (c i) t -> p c t i", i=4)
-                src = wide[s][:].rearrange("p t (c i) -> p c t i", i=4)
+                dst = gt[:].rearrange("p (c i) t -> p c t i", i=8)
+                src = wide[s][:].rearrange("p t (c i) -> p c t i", i=8)
             else:
                 dst = gt[:]
                 src = wide[s][:].rearrange("p t n -> p n t")
@@ -215,9 +215,9 @@ def tile_lorasequential_pa_kernel(tc, x, h_lora, lora_B, M_bytes, M_scale, out):
             w = WIDTHS[u // N_M]
             l = work.tile([P, w], F32, name="lo", tag="lo", bufs=10)
             if l_vec[u]:
-                nc.vector.tensor_scalar(out=l[:], in0=lps[u][:], scalar1=2.0, scalar2=None, op0=MULT)
+                nc.vector.tensor_copy(out=l[:], in_=lps[u][:])
             else:
-                nc.scalar.activation(out=l[:], in_=lps[u][:], func=COPY, scale=2.0)
+                nc.scalar.copy(out=l[:], in_=lps[u][:])
             lo[u] = l
 
         def parts(u):
@@ -242,7 +242,7 @@ def tile_lorasequential_pa_kernel(tc, x, h_lora, lora_B, M_bytes, M_scale, out):
             j, m = divmod(u, N_M)
             l = lo[u]
             for c in parts(u):
-                nc.vector.tensor_tensor(out=l[:, c], in0=acc[u][:, c], in1=l[:, c], op=ADD)
+                nc.vector.scalar_tensor_tensor(out=l[:, c], in0=l[:, c], scalar=2.0, in1=acc[u][:, c], op0=MULT, op1=ADD)
                 nc.sync.dma_start(out=out[m * P:(m + 1) * P, offs[j] + c.start:offs[j] + c.stop], in_=l[:, c])
 
         need = []

from contextlib import ExitStack

import concourse.mybir as mybir
from concourse.masks import make_identity

BATCH, IN_F, OUT_F, RANK, N_AD = 1024, 2048, 2048, 128, 8
FLOPS = 2 * BATCH * IN_F * OUT_F + 2 * BATCH * RANK * OUT_F

F32 = mybir.dt.float32
BF16 = mybir.dt.bfloat16
U32 = mybir.dt.uint32
U8 = mybir.dt.uint8
FP8 = mybir.dt.float8_e4m3fn
FP8X4 = mybir.dt.float8_e4m3fn_x4
COPY = mybir.ActivationFunctionType.Copy
MULT = mybir.AluOpType.mult
ADD = mybir.AluOpType.add

P = 128
PACK = 4
K_PASS = P * PACK
N_PASS = IN_F // K_PASS
LW = 512
N_M = BATCH // P

WIDTHS = (512, 512, 512, 256, 256)
V_PLANES = (8, 4, 0, 0, 2)
S_INTER = (0, 0, 0, 0, 0)
X_EVAC_V = 0
L_EVAC_V = (0, 0, 0, 0, 0)
SH_S = 3
SH_V = 1
X_LEAD = 4
LAG_LE = 1
LAG_F = 2
D_LEAD = {"m": 6, "x": 6, "b": 5, "h": 6}
M_LATE = (0, 2, 0, 0, 0)
L_LATE = 4
B_SPLIT = 2
FAST_INTER = True
MANUAL = True
WARM_X = (2, 3, 4,)


def spread(total, n):
    return [(total * (i + 1)) // n - (total * i) // n for i in range(n)]


def tile_lorasequential_pa_kernel(tc, x, h_lora, lora_B, M_bytes, M_scale, out):
    nc = tc.nc
    n_ch = len(WIDTHS)
    n_u = N_M * n_ch
    offs = [sum(WIDTHS[:i]) for i in range(n_ch)]
    v_plane = []
    s_int = []
    l_vec = []
    for j in range(n_ch):
        v_plane.extend(spread(V_PLANES[j], N_PASS * PACK))
        s_int.extend(spread(S_INTER[j], N_PASS))
        l_vec.extend(spread(L_EVAC_V[j], N_M))
    x_vec = spread(X_EVAC_V, 2 * N_M)
    with ExitStack() as ctx:
        const = ctx.enter_context(tc.tile_pool(name="const", bufs=1))
        loads = ctx.enter_context(tc.tile_pool(name="loads", bufs=1))
        codes = ctx.enter_context(tc.tile_pool(name="codes", bufs=1))
        work = ctx.enter_context(tc.tile_pool(name="work", bufs=3))
        psum = ctx.enter_context(tc.psum_pool(name="psum", bufs=4))
        if MANUAL:
            ctx.enter_context(tc.manual_schedule())

        ident_f = const.tile([P, P], F32, name="ident_f")
        make_identity(nc, ident_f[:])
        ident_b = const.tile([P, P], BF16, name="ident_b")
        make_identity(nc, ident_b[:])
        warm = const.tile([P, 2], F32, name="warm")
        nc.vector.memset(warm[:, 0:1], 0.0)
        nc.scalar.activation(out=warm[:, 1:2], in_=warm[:, 0:1], func=COPY)

        msc_first = const.tile([P, PACK], F32, name="msc_first")
        msc_rest = const.tile([P, N_PASS - 1, PACK], F32, name="msc_rest")
        sc_view = M_scale.rearrange("(g p t) o -> p g (t o)", p=P, t=PACK)
        nc.sync.dma_start(out=msc_first[:], in_=sc_view[:, 0, :])
        m_view = M_bytes.rearrange("(g p t) n -> g p t n", p=P, t=PACK)
        b_view = lora_B.rearrange("a r n -> r a n")
        mb = {}
        xin = {}
        lb = {}
        hin = loads.tile([P, N_AD, RANK], BF16, name="hin")
        hT = codes.tile([P, N_AD, P], BF16, name="hT")

        def load(item):
            kind = item[0]
            if kind == "m":
                jl, g = item[1], item[2]
                n = PACK // 2 if jl == 0 else PACK
                for t0 in range(0, PACK, n):
                    t = loads.tile([P, n, LW], U8, name="mb%d_%d_%d" % (jl, g, t0))
                    nc.sync.dma_start(out=t[:], in_=m_view[g][:, t0:t0 + n, jl * LW:(jl + 1) * LW])
                    for i in range(n):
                        mb[(jl, g, t0 + i)] = t[:, i, :]
                if (jl, g) == (0, 0):
                    nc.sync.dma_start(out=msc_rest[:], in_=sc_view[:, 1:, :])
            elif kind == "x":
                m = item[1]
                t = loads.tile([P, IN_F], BF16, name="xin%d" % m)
                nc.sync.dma_start(out=t[:], in_=x[m * P:(m + 1) * P, :])
                xin[m] = t
            elif kind == "b":
                jl, a0 = item[1], item[2]
                t = loads.tile([P, B_SPLIT, LW], BF16, name="lb%d_%d" % (jl, a0))
                nc.sync.dma_start(out=t[:], in_=b_view[:, a0:a0 + B_SPLIT, jl * LW:(jl + 1) * LW])
                lb[(jl, a0)] = t
            else:
                nc.sync.dma_start(out=hin[:], in_=h_lora.rearrange("a b r -> b a r"))

        wide = {}
        grp = {}
        mc = {}
        ms = {}
        xc = {}
        xs = {}
        xg = {}
        tps = {}
        lps = {}
        lo = {}
        acc = {}

        def wid(s, t):
            j, g = divmod(s, N_PASS)
            w = WIDTHS[j]
            jl, c0 = divmod(offs[j], LW)
            if s not in wide:
                wt = work.tile([P, PACK, w], BF16, name="wide", tag="wide", bufs=3)
                wide[s] = wt
            dst = wide[s][:, t, :]
            src = mb[(jl, g, t)][:, c0:c0 + w].bitcast(FP8)
            scale = msc_first[:, t:t + 1] if g == 0 else msc_rest[:, g - 1, t:t + 1]
            if v_plane[j * N_PASS * PACK + g * PACK + t]:
                nc.vector.tensor_scalar(out=dst, in0=src, scalar1=scale, scalar2=None, op0=MULT)
            else:
                nc.scalar.activation(out=dst, in_=src, func=COPY, scale=scale)

        def itl(s):
            w = WIDTHS[s // N_PASS]
            gt = work.tile([P, w, PACK], BF16, name="grp", tag="grp", bufs=3, align_bytes=64)
            if FAST_INTER:
                dst = gt[:].rearrange("p (c i) t -> p c t i", i=8)
                src = wide[s][:].rearrange("p t (c i) -> p c t i", i=8)
            else:
                dst = gt[:]
                src = wide[s][:].rearrange("p t n -> p n t")
            if s_int[s]:
                nc.scalar.copy(out=dst, in_=src)
            else:
                nc.vector.tensor_copy(out=dst, in_=src)
            grp[s] = gt

        def qnt(s):
            w = WIDTHS[s // N_PASS]
            c = codes.tile([P, w], U32, name="mc%d" % s, align_bytes=64)
            sc = codes.tile([P, w], U8, name="ms%d" % s, align_bytes=64)
            nc.vector.quantize_mx(out=c[:].bitcast(FP8X4), scales=sc[:],
                                  in_=grp[s][:].rearrange("p n t -> p (n t)"))
            mc[s] = c
            ms[s] = sc

        def warm_pe(m):
            for i in range(2):
                d = psum.tile([P, LW], F32, name="wp", tag="acc", bufs=4)
                nc.tensor.matmul(d[:], lhsT=ident_b[:], rhs=xin[m - 1][:, i * LW:(i + 1) * LW], start=True, stop=True)

        def x_tr(m, hh):
            words = xin[m][:].bitcast(F32)
            tp = psum.tile([P, 2, 2, P], F32, name="tp", tag="aux", bufs=4)
            for gi in range(2):
                g = 2 * hh + gi
                for u in range(2):
                    nc.tensor.transpose(tp[:, gi, u, :], words[:, 256 * g + u:256 * (g + 1):2], ident_f[:])
            tps[(m, hh)] = tp

        def x_ev(m, hh):
            if m not in xg:
                gw = work.tile([P, N_PASS, P, 2], F32, name="xg", tag="xg", bufs=4, align_bytes=64)
                xg[m] = gw
            dst = xg[m][:, 2 * hh:2 * hh + 2, :, :]
            src = tps[(m, hh)][:].rearrange("p g u r -> p g r u")
            if x_vec[2 * m + hh]:
                nc.vector.tensor_copy(out=dst, in_=src)
            else:
                nc.scalar.copy(out=dst, in_=src)

        def x_q(m):
            c = codes.tile([P, N_PASS * P], U32, name="xc%d" % m, align_bytes=64)
            sc = codes.tile([P, N_PASS * P], U8, name="xs%d" % m, align_bytes=64)
            nc.vector.quantize_mx(out=c[:].bitcast(FP8X4), scales=sc[:],
                                  in_=xg[m][:].rearrange("p g r u -> p (g r u)").bitcast(BF16))
            xc[m] = c
            xs[m] = sc

        def h_tr():
            tp = psum.tile([P, N_AD, P], BF16, name="tph", tag="aux", bufs=4)
            for a in range(N_AD):
                nc.tensor.transpose(tp[:, a, :], hin[:, a, :], ident_b[:])
            nc.vector.tensor_copy(out=hT[:], in_=tp[:])

        def l_mm(u):
            j, m = divmod(u, N_M)
            w = WIDTHS[j]
            jl, c0 = divmod(offs[j], LW)
            lp = psum.tile([P, w], F32, name="lp", tag="aux", bufs=4)
            nc.tensor.matmul(lp[:], lhsT=hT[:, m, :], rhs=lb[(jl, m - m % B_SPLIT)][:, m % B_SPLIT, c0:c0 + w], start=True, stop=True)
            lps[u] = lp

        def l_ev(u):
            w = WIDTHS[u // N_M]
            l = work.tile([P, w], F32, name="lo", tag="lo", bufs=10)
            if l_vec[u]:
                nc.vector.tensor_copy(out=l[:], in_=lps[u][:])
            else:
                nc.scalar.copy(out=l[:], in_=lps[u][:])
            lo[u] = l

        def parts(u):
            w = WIDTHS[u // N_M]
            n = w // 2 if u == n_u - 1 else w
            return [slice(c, c + n) for c in range(0, w, n)]

        def mx(u):
            j, m = divmod(u, N_M)
            a = psum.tile([P, WIDTHS[j]], F32, name="acc", tag="acc", bufs=4)
            for c in parts(u):
                for g in range(N_PASS):
                    s = j * N_PASS + g
                    cols = slice(g * P, (g + 1) * P)
                    nc.tensor.matmul_mx(out=a[:, c],
                                        lhsT=xc[m][:, cols].bitcast(FP8X4), lhsT_scale=xs[m][:, cols],
                                        rhs=mc[s][:, c].bitcast(FP8X4), rhs_scale=ms[s][:, c],
                                        start=(g == 0), stop=(g == N_PASS - 1))
            acc[u] = a

        def fin(u):
            j, m = divmod(u, N_M)
            l = lo[u]
            for c in parts(u):
                nc.vector.scalar_tensor_tensor(out=l[:, c], in0=l[:, c], scalar=2.0, in1=acc[u][:, c], op0=MULT, op1=ADD)
                nc.sync.dma_start(out=out[m * P:(m + 1) * P, offs[j] + c.start:offs[j] + c.stop], in_=l[:, c])

        need = []
        for j in range(n_ch):
            for g in range(N_PASS):
                need.append((N_M * j + 2 * g - N_M - SH_S - D_LEAD["m"] + M_LATE[j], 0, ("m", offs[j] // LW, g)))
            for a0 in range(0, N_AD, B_SPLIT):
                need.append((N_M * j + a0 - D_LEAD["b"], 2, ("b", offs[j] // LW, a0)))
        for m in range(N_M):
            need.append((m - X_LEAD - D_LEAD["x"], 1, ("x", m)))
        need.append((-D_LEAD["h"], 1, ("h",)))
        sched = []
        seen = set()
        for slot, rank, item in sorted(need, key=lambda z: (z[0], z[1])):
            if item not in seen:
                seen.add(item)
                sched.append((slot, item))

        first = min(-N_M - SH_S, -X_LEAD)
        n_loaded = 0
        for sl in range(first, n_u + LAG_F + LAG_LE):
            while n_loaded < len(sched) and sched[n_loaded][0] <= sl:
                load(sched[n_loaded][1])
                n_loaded += 1
            m = sl + X_LEAD
            if 0 <= m < N_M:
                if m in WARM_X:
                    warm_pe(m)
                x_tr(m, 0)
                x_tr(m, 1)
            if 0 <= sl - 1 < L_LATE:
                l_mm(sl - 1)
            if L_LATE <= sl < n_u:
                l_mm(sl)
            if 0 <= sl < n_u:
                mx(sl)
            if sl == 0:
                h_tr()
            if 0 <= m < N_M:
                x_ev(m, 0)
                x_ev(m, 1)
            if 0 <= sl - LAG_LE < n_u:
                l_ev(sl - LAG_LE)
            if 0 <= sl - LAG_F < n_u:
                fin(sl - LAG_F)
            q = sl + N_M + SH_S
            if 0 <= q < n_u:
                j, i = divmod(q, N_M)
                wid(N_PASS * j + i // 2, 2 * (i % 2))
                wid(N_PASS * j + i // 2, 2 * (i % 2) + 1)
            q = sl + N_M + SH_V
            if 0 <= q < n_u:
                j, i = divmod(q, N_M)
                if i % 2 == 0:
                    itl(N_PASS * j + i // 2)
                else:
                    qnt(N_PASS * j + i // 2)
            if 0 <= m - 1 < N_M:
                x_q(m - 1)
